import numpy as np
import ml_dtypes


def mxq(x, axis, fmt="e4m3"):
    dtype, down = {"e4m3": (ml_dtypes.float8_e4m3fn, 7), "e5m2": (ml_dtypes.float8_e5m2, 14)}[fmt]
    v = np.moveaxis(np.asarray(x, np.float32).astype(ml_dtypes.bfloat16).astype(np.float64), axis, -1)
    blocks = v.reshape(v.shape[:-1] + (-1, 32))
    amax = np.abs(blocks).max(-1, keepdims=True)
    byte = np.maximum(np.where(amax > 0, np.frexp(amax)[1] - 1 + 127, 0) - down, 1)
    scale = np.exp2(byte - 127.0)
    codes = (blocks / scale).astype(np.float32).astype(dtype).astype(np.float64)
    return np.moveaxis((codes * scale).reshape(v.shape), -1, axis)


WIDE = False


def mx_kscale(k):
    if not WIDE:
        return np.ones(k)
    levels = np.array([20, -20, 10, -10, 0])
    a = np.random.permutation(np.resize(levels, k // 512 * 4)).reshape(k // 512, 4)
    idx = np.arange(k)
    return np.exp2(a[idx // 512, idx % 128 // 32])


BF16 = ml_dtypes.bfloat16


def bf(x):
    return np.asarray(x, np.float32).astype(BF16)


def f64(x):
    return np.asarray(x).astype(np.float64)


B, H, W, CIN, COUT = 1024, 2, 2, 512, 512
P = H * W


def setup_inputs():
    s = mx_kscale(B)[:, None, None, None]
    inputs = np.random.standard_normal((B, H, W, CIN)) * s
    kernel = np.random.standard_normal((H, W, CIN, H, W, COUT)) / np.sqrt(CIN)
    bias = np.random.standard_normal((H, W, COUT)) * 0.5
    g = np.random.standard_normal((B, H, W, COUT)) * np.exp2(np.random.randint(-12, 1, (B, H, W, 1))) / s
    return {"inputs": bf(inputs), "kernel": bf(kernel), "bias": bf(bias), "grad_out": bf(g)}


def reference(inputs, kernel, bias, grad_out):
    x = f64(inputs).reshape(B, P, CIN).transpose(1, 0, 2)
    g = f64(grad_out).reshape(B, P, COUT).transpose(1, 0, 2)
    d = mxq(x, 1, "e4m3").transpose(0, 2, 1) @ mxq(g, 1, "e5m2")
    out = np.zeros((P, CIN, P, COUT))
    idx = np.arange(P)
    out[idx, :, idx, :] = d
    return out.reshape(H, W, CIN, H, W, COUT)

@@ -1,0 +1,110 @@
+from contextlib import ExitStack
+
+import concourse.mybir as mybir
+
+B = 1024
+PLACES = 4
+C = 512
+FLOPS = 2 * PLACES * C * C * B
+BYTES = 2 * B * PLACES * C * 2 + (PLACES * C) * (PLACES * C) * 4
+
+BF16 = mybir.dt.bfloat16
+F32 = mybir.dt.float32
+U32 = mybir.dt.uint32
+U8 = mybir.dt.uint8
+E4M3X4 = mybir.dt.float8_e4m3fn_x4
+E5M2X4 = mybir.dt.float8_e5m2_x4
+
+P = 128
+PACK = 4
+K_PASS = P * PACK
+PASSES = B // K_PASS
+M_TILES = C // P
+W = PLACES * C
+
+
+def tile_locallyconnected2d_kernel(tc, inputs, kernel, bias, grad_out, out):
+    nc = tc.nc
+    x2 = inputs.rearrange("b h w c -> b (h w c)")
+    g2 = grad_out.rearrange("b h w c -> b (h w c)")
+    out2 = out.rearrange("a b c d e f -> (a b c) (d e f)")
+    with ExitStack() as ctx:
+        keep = ctx.enter_context(tc.tile_pool(name="keep", bufs=1))
+        stage = ctx.enter_context(tc.tile_pool(name="stage", bufs=4))
+        psum = ctx.enter_context(tc.psum_pool(name="psum", bufs=8))
+        ctx.enter_context(tc.manual_schedule())
+
+        raw = {}
+        for c in range(PASSES):
+            for who, src in (("x", x2), ("g", g2)):
+                t = keep.tile([P, PACK, W], BF16, name="raw_%s%d" % (who, c))
+                nc.sync.dma_start(
+                    out=t[:],
+                    in_=src[c * K_PASS : (c + 1) * K_PASS, :].rearrange("(p j) w -> p j w", j=PACK),
+                )
+                raw[(who, c)] = t
+
+        zeros = keep.tile([P, M_TILES, 3 * C], F32, name="zeros")
+        nc.vector.memset(zeros[:], 0.0)
+        for pl in range(PLACES):
+            rows = out2[pl * C : (pl + 1) * C, :].rearrange("(t m) f -> m t f", m=P)
+            if pl > 0:
+                nc.sync.dma_start(out=rows[:, :, 0 : pl * C], in_=zeros[:, :, 0 : pl * C])
+            if pl < PLACES - 1:
+                nc.sync.dma_start(
+                    out=rows[:, :, (pl + 1) * C : W], in_=zeros[:, :, 0 : (PLACES - 1 - pl) * C]
+                )
+
+        units = [(who, c, pl) for c in range(PASSES) for who in ("x", "g") for pl in range(PLACES)]
+        grouped = {}
+        codes = {}
+        scales = {}
+
+        def regroup(u):
+            who, c, pl = u
+            gr = stage.tile([P, C, PACK], BF16, name="grouped", align_bytes=64)
+            nc.vector.tensor_copy(
+                out=gr[:].rearrange("p (c i) t -> p c t i", i=4),
+                in_=raw[(who, c)][:, :, pl * C : (pl + 1) * C].rearrange("p t (c i) -> p c t i", i=4),
+            )
+            grouped[u] = gr
+
+        def quantise(u):
+            who, c, pl = u
+            cd = keep.tile([P, C], U32, name="codes_%s%d%d" % u, align_bytes=64)
+            sc = keep.tile([P, C], U8, name="scales_%s%d%d" % u, align_bytes=64)
+            nc.vector.quantize_mx(
+                out=cd[:].bitcast(E4M3X4 if who == "x" else E5M2X4),
+                scales=sc[:],
+                in_=grouped[u][:].rearrange("p w j -> p (w j)"),
+            )
+            codes[u] = cd
+            scales[u] = sc
+
+        def place(pl):
+            res = keep.tile([P, M_TILES, C], F32, name="res_%d" % pl)
+            for mt in range(M_TILES):
+                acc = psum.tile([P, C], F32, name="acc")
+                for c in range(PASSES):
+                    nc.tensor.matmul_mx(
+                        out=acc[:],
+                        lhsT=codes[("x", c, pl)][:, mt * P : (mt + 1) * P].bitcast(E4M3X4),
+                        lhsT_scale=scales[("x", c, pl)][:, mt * P : (mt + 1) * P],
+                        rhs=codes[("g", c, pl)][:].bitcast(E5M2X4),
+                        rhs_scale=scales[("g", c, pl)][:],
+                        start=(c == 0),
+                        stop=(c == PASSES - 1),
+                    )
+                nc.scalar.copy(out=res[:, mt, :], in_=acc[:])
+            nc.sync.dma_start(
+                out=out2[pl * C : (pl + 1) * C, pl * C : (pl + 1) * C].rearrange("(t m) f -> m t f", m=P),
+                in_=res[:],
+            )
+
+        regroup(units[0])
+        for i, u in enumerate(units):
+            if i + 1 < len(units):
+                regroup(units[i + 1])
+            quantise(u)
+            if u[0] == "g" and u[1] == PASSES - 1:
+                place(u[2])

@@ -10,6 +10,7 @@ BYTES = 2 * B * PLACES * C * 2 + (PLACES * C) * (PLACES * C) * 4
 
 BF16 = mybir.dt.bfloat16
 F32 = mybir.dt.float32
+I32 = mybir.dt.int32
 U32 = mybir.dt.uint32
 U8 = mybir.dt.uint8
 E4M3X4 = mybir.dt.float8_e4m3fn_x4
@@ -21,6 +22,15 @@ K_PASS = P * PACK
 PASSES = B // K_PASS
 M_TILES = C // P
 W = PLACES * C
+
+UNITS = [
+    ("x", 0, 3), ("x", 0, 2), ("x", 0, 1), ("x", 0, 0),
+    ("g", 0, 3), ("g", 0, 2), ("g", 0, 1),
+    ("x", 1, 3), ("g", 1, 3),
+    ("x", 1, 2), ("g", 1, 2),
+    ("x", 1, 1), ("g", 1, 1),
+    ("g", 0, 0), ("x", 1, 0), ("g", 1, 0),
+]
 
 
 def tile_locallyconnected2d_kernel(tc, inputs, kernel, bias, grad_out, out):
@@ -44,27 +54,35 @@ def tile_locallyconnected2d_kernel(tc, inputs, kernel, bias, grad_out, out):
                 )
                 raw[(who, c)] = t
 
-        zeros = keep.tile([P, M_TILES, 3 * C], F32, name="zeros")
-        nc.vector.memset(zeros[:], 0.0)
-        for pl in range(PLACES):
-            rows = out2[pl * C : (pl + 1) * C, :].rearrange("(t m) f -> m t f", m=P)
-            if pl > 0:
-                nc.sync.dma_start(out=rows[:, :, 0 : pl * C], in_=zeros[:, :, 0 : pl * C])
-            if pl < PLACES - 1:
-                nc.sync.dma_start(
-                    out=rows[:, :, (pl + 1) * C : W], in_=zeros[:, :, 0 : (PLACES - 1 - pl) * C]
-                )
+        def out_rows(pl):
+            return out2[pl * C : (pl + 1) * C, :].rearrange("(m t) f -> m t f", t=M_TILES)
 
-        units = [(who, c, pl) for c in range(PASSES) for who in ("x", "g") for pl in range(PLACES)]
+        frame = {}
+        for pl in (3, 2, 1):
+            frame[pl] = keep.tile([P, M_TILES, W], F32, name="frame_%d" % pl)
+        nc.vector.memset(frame[3][:, :, 0 : 3 * C].bitcast(I32), 0)
+        nc.scalar.copy(out=frame[2][:, :, 0 : 2 * C], in_=frame[3][:, :, 0 : 2 * C])
+        nc.scalar.copy(out=frame[2][:, :, 3 * C : W], in_=frame[3][:, :, 0:C])
+        nc.scalar.copy(out=frame[1][:, :, 0:C], in_=frame[3][:, :, 0:C])
+        nc.scalar.copy(out=frame[1][:, :, 2 * C : W], in_=frame[3][:, :, 0 : 2 * C])
+        res0 = keep.tile([P, M_TILES, C], F32, name="res0")
+
+        nc.sync.dma_start(out=out_rows(0)[:, :, C:W], in_=frame[3][:, :, 0 : 3 * C])
+
         grouped = {}
         codes = {}
         scales = {}
+        acc = {}
 
         def regroup(u):
             who, c, pl = u
             gr = stage.tile([P, C, PACK], BF16, name="grouped", align_bytes=64)
+            if who == "x":
+                dst = gr[:].rearrange("p (i c) t -> p c t i", i=4)
+            else:
+                dst = gr[:].rearrange("p (c i) t -> p c t i", i=4)
             nc.vector.tensor_copy(
-                out=gr[:].rearrange("p (c i) t -> p c t i", i=4),
+                out=dst,
                 in_=raw[(who, c)][:, :, pl * C : (pl + 1) * C].rearrange("p t (c i) -> p c t i", i=4),
             )
             grouped[u] = gr
@@ -81,30 +99,57 @@ def tile_locallyconnected2d_kernel(tc, inputs, kernel, bias, grad_out, out):
             codes[u] = cd
             scales[u] = sc
 
-        def place(pl):
-            res = keep.tile([P, M_TILES, C], F32, name="res_%d" % pl)
-            for mt in range(M_TILES):
-                acc = psum.tile([P, C], F32, name="acc")
-                for c in range(PASSES):
-                    nc.tensor.matmul_mx(
-                        out=acc[:],
-                        lhsT=codes[("x", c, pl)][:, mt * P : (mt + 1) * P].bitcast(E4M3X4),
-                        lhsT_scale=scales[("x", c, pl)][:, mt * P : (mt + 1) * P],
-                        rhs=codes[("g", c, pl)][:].bitcast(E5M2X4),
-                        rhs_scale=scales[("g", c, pl)][:],
-                        start=(c == 0),
-                        stop=(c == PASSES - 1),
-                    )
-                nc.scalar.copy(out=res[:, mt, :], in_=acc[:])
-            nc.sync.dma_start(
-                out=out2[pl * C : (pl + 1) * C, pl * C : (pl + 1) * C].rearrange("(t m) f -> m t f", m=P),
-                in_=res[:],
+        def mx_pass(pl, mt, c):
+            if c == 0:
+                acc[(pl, mt)] = psum.tile([P, C], F32, name="acc")
+            nc.tensor.matmul_mx(
+                out=acc[(pl, mt)][:],
+                lhsT=codes[("x", c, pl)][:, mt * P : (mt + 1) * P].bitcast(E4M3X4),
+                lhsT_scale=scales[("x", c, pl)][:, mt * P : (mt + 1) * P],
+                rhs=codes[("g", c, pl)][:].bitcast(E5M2X4),
+                rhs_scale=scales[("g", c, pl)][:],
+                start=(c == 0),
+                stop=(c == PASSES - 1),
             )
 
-        regroup(units[0])
-        for i, u in enumerate(units):
-            if i + 1 < len(units):
-                regroup(units[i + 1])
-            quantise(u)
-            if u[0] == "g" and u[1] == PASSES - 1:
-                place(u[2])
+        def evacuate(pl, mt):
+            if pl == 0:
+                dst = res0[:, mt, :]
+            else:
+                dst = frame[pl][:, mt, pl * C : (pl + 1) * C]
+            nc.scalar.copy(out=dst, in_=acc[(pl, mt)][:])
+
+        def finish(pl):
+            for mt in range(M_TILES):
+                if pl != 3:
+                    mx_pass(pl, mt, 0)
+                mx_pass(pl, mt, 1)
+                evacuate(pl, mt)
+                if pl == 3 and mt % 2 == 1:
+                    nc.sync.dma_start(
+                        out=out_rows(pl)[:, mt - 1 : mt + 1, :], in_=frame[pl][:, mt - 1 : mt + 1, :]
+                    )
+            if pl == 0:
+                nc.sync.dma_start(out=out_rows(0)[:, :, 0:C], in_=res0[:])
+            elif pl != 3:
+                nc.sync.dma_start(
+                    out=out_rows(pl).rearrange("m t f -> m (t f)"),
+                    in_=frame[pl][:].rearrange("p t f -> p (t f)"),
+                )
+
+        def after(u):
+            if u == ("g", 0, 3):
+                for mt in range(M_TILES):
+                    mx_pass(3, mt, 0)
+            if u[0] == "g" and u[1] == 1:
+                finish(u[2])
+
+        n = len(UNITS)
+        regroup(UNITS[0])
+        for i in range(n):
+            if i + 1 < n and UNITS[i] != ("g", 1, 3):
+                regroup(UNITS[i + 1])
+            quantise(UNITS[i])
+            after(UNITS[i])
+            if UNITS[i] == ("g", 1, 3):
+                regroup(UNITS[i + 1])

@@ -24,13 +24,15 @@ M_TILES = C // P
 W = PLACES * C
 
 UNITS = [
-    ("x", 0, 3), ("x", 0, 2), ("x", 0, 1), ("x", 0, 0),
-    ("g", 0, 3), ("g", 0, 2), ("g", 0, 1),
-    ("x", 1, 3), ("g", 1, 3),
-    ("x", 1, 2), ("g", 1, 2),
-    ("x", 1, 1), ("g", 1, 1),
-    ("g", 0, 0), ("x", 1, 0), ("g", 1, 0),
+    ("x", 0, 3), ("x", 0, 2), ("x", 0, 1),
+    ("g", 0, 3), ("g", 0, 2),
+    ("g", 1, 3), ("g", 1, 2),
+    ("x", 1, 3),
+    ("x", 1, 2),
+    ("g", 0, 1), ("g", 1, 1), ("x", 1, 1),
+    ("x", 0, 0), ("g", 0, 0), ("g", 1, 0), ("x", 1, 0),
 ]
+LOADS = [("x", 0), ("g", 0), ("g", 1), ("x", 1)]
 
 
 def tile_locallyconnected2d_kernel(tc, inputs, kernel, bias, grad_out, out):
@@ -40,19 +42,20 @@ def tile_locallyconnected2d_kernel(tc, inputs, kernel, bias, grad_out, out):
     out2 = out.rearrange("a b c d e f -> (a b c) (d e f)")
     with ExitStack() as ctx:
         keep = ctx.enter_context(tc.tile_pool(name="keep", bufs=1))
-        stage = ctx.enter_context(tc.tile_pool(name="stage", bufs=4))
+        stage = ctx.enter_context(tc.tile_pool(name="stage", bufs=3))
+        small = ctx.enter_context(tc.tile_pool(name="small", bufs=4))
         psum = ctx.enter_context(tc.psum_pool(name="psum", bufs=8))
         ctx.enter_context(tc.manual_schedule())
 
         raw = {}
-        for c in range(PASSES):
-            for who, src in (("x", x2), ("g", g2)):
-                t = keep.tile([P, PACK, W], BF16, name="raw_%s%d" % (who, c))
-                nc.sync.dma_start(
-                    out=t[:],
-                    in_=src[c * K_PASS : (c + 1) * K_PASS, :].rearrange("(p j) w -> p j w", j=PACK),
-                )
-                raw[(who, c)] = t
+        for who, c in LOADS:
+            src = x2 if who == "x" else g2
+            t = keep.tile([P, PACK, W], BF16, name="raw_%s%d" % (who, c))
+            nc.sync.dma_start(
+                out=t[:],
+                in_=src[c * K_PASS : (c + 1) * K_PASS, :].rearrange("(p j) w -> p j w", j=PACK),
+            )
+            raw[(who, c)] = t
 
         def out_rows(pl):
             return out2[pl * C : (pl + 1) * C, :].rearrange("(m t) f -> m t f", t=M_TILES)
@@ -99,13 +102,36 @@ def tile_locallyconnected2d_kernel(tc, inputs, kernel, bias, grad_out, out):
             codes[u] = cd
             scales[u] = sc
 
+        def regroup_tile(mt):
+            gs = small.tile([P, P, PACK], BF16, name="grouped_s", align_bytes=64)
+            nc.vector.tensor_copy(
+                out=gs[:],
+                in_=raw[("x", 1)][:, :, 3 * C : W].rearrange("p j (m i) -> p i m j", i=4)[:, mt, :, :],
+            )
+            grouped[mt] = gs
+
+        def quantise_tile(mt):
+            cd = keep.tile([P, P], U32, name="codes_t%d" % mt, align_bytes=64)
+            sc = keep.tile([P, P], U8, name="scales_t%d" % mt, align_bytes=64)
+            nc.vector.quantize_mx(
+                out=cd[:].bitcast(E4M3X4), scales=sc[:], in_=grouped[mt][:].rearrange("p w j -> p (w j)")
+            )
+            codes[mt] = cd
+            scales[mt] = sc
+
         def mx_pass(pl, mt, c):
             if c == 0:
                 acc[(pl, mt)] = psum.tile([P, C], F32, name="acc")
+            if (c, pl) == (1, 3):
+                lhs = codes[mt][:]
+                lhs_scale = scales[mt][:]
+            else:
+                lhs = codes[("x", c, pl)][:, mt * P : (mt + 1) * P]
+                lhs_scale = scales[("x", c, pl)][:, mt * P : (mt + 1) * P]
             nc.tensor.matmul_mx(
                 out=acc[(pl, mt)][:],
-                lhsT=codes[("x", c, pl)][:, mt * P : (mt + 1) * P].bitcast(E4M3X4),
-                lhsT_scale=scales[("x", c, pl)][:, mt * P : (mt + 1) * P],
+                lhsT=lhs.bitcast(E4M3X4),
+                lhsT_scale=lhs_scale,
                 rhs=codes[("g", c, pl)][:].bitcast(E5M2X4),
                 rhs_scale=scales[("g", c, pl)][:],
                 start=(c == 0),
@@ -119,19 +145,22 @@ def tile_locallyconnected2d_kernel(tc, inputs, kernel, bias, grad_out, out):
                 dst = frame[pl][:, mt, pl * C : (pl + 1) * C]
             nc.scalar.copy(out=dst, in_=acc[(pl, mt)][:])
 
+        def finish_tile(pl, mt):
+            if pl != 3:
+                mx_pass(pl, mt, 0)
+            mx_pass(pl, mt, 1)
+            evacuate(pl, mt)
+            if pl == 3 and mt % 2 == 1:
+                nc.sync.dma_start(
+                    out=out_rows(pl)[:, mt - 1 : mt + 1, :], in_=frame[pl][:, mt - 1 : mt + 1, :]
+                )
+
         def finish(pl):
             for mt in range(M_TILES):
-                if pl != 3:
-                    mx_pass(pl, mt, 0)
-                mx_pass(pl, mt, 1)
-                evacuate(pl, mt)
-                if pl == 3 and mt % 2 == 1:
-                    nc.sync.dma_start(
-                        out=out_rows(pl)[:, mt - 1 : mt + 1, :], in_=frame[pl][:, mt - 1 : mt + 1, :]
-                    )
+                finish_tile(pl, mt)
             if pl == 0:
                 nc.sync.dma_start(out=out_rows(0)[:, :, 0:C], in_=res0[:])
-            elif pl != 3:
+            else:
                 nc.sync.dma_start(
                     out=out_rows(pl).rearrange("m t f -> m (t f)"),
                     in_=frame[pl][:].rearrange("p t f -> p (t f)"),
@@ -141,15 +170,23 @@ def tile_locallyconnected2d_kernel(tc, inputs, kernel, bias, grad_out, out):
             if u == ("g", 0, 3):
                 for mt in range(M_TILES):
                     mx_pass(3, mt, 0)
-            if u[0] == "g" and u[1] == 1:
+            if u[0] == "x" and u[1] == 1:
                 finish(u[2])
 
-        n = len(UNITS)
-        regroup(UNITS[0])
-        for i in range(n):
-            if i + 1 < n and UNITS[i] != ("g", 1, 3):
-                regroup(UNITS[i + 1])
-            quantise(UNITS[i])
-            after(UNITS[i])
-            if UNITS[i] == ("g", 1, 3):
-                regroup(UNITS[i + 1])
+        def run(units):
+            regroup(units[0])
+            for i, u in enumerate(units):
+                if i + 1 < len(units):
+                    regroup(units[i + 1])
+                quantise(u)
+                after(u)
+
+        cut = UNITS.index(("x", 1, 3))
+        run(UNITS[:cut])
+        regroup_tile(0)
+        for mt in range(M_TILES):
+            if mt + 1 < M_TILES:
+                regroup_tile(mt + 1)
+            quantise_tile(mt)
+            finish_tile(3, mt)
+        run(UNITS[cut + 1 :])

@@ -24,12 +24,12 @@ M_TILES = C // P
 W = PLACES * C
 
 UNITS = [
-    ("x", 0, 3), ("x", 0, 2), ("x", 0, 1),
+    ("x", 0, 3), ("x", 0, 2),
     ("g", 0, 3), ("g", 0, 2),
     ("g", 1, 3), ("g", 1, 2),
     ("x", 1, 3),
     ("x", 1, 2),
-    ("g", 0, 1), ("g", 1, 1), ("x", 1, 1),
+    ("x", 0, 1), ("g", 0, 1), ("g", 1, 1), ("x", 1, 1),
     ("x", 0, 0), ("g", 0, 0), ("g", 1, 0), ("x", 1, 0),
 ]
 LOADS = [("x", 0), ("g", 0), ("g", 1), ("x", 1)]
@@ -150,10 +150,9 @@ def tile_locallyconnected2d_kernel(tc, inputs, kernel, bias, grad_out, out):
                 mx_pass(pl, mt, 0)
             mx_pass(pl, mt, 1)
             evacuate(pl, mt)
-            if pl == 3 and mt % 2 == 1:
-                nc.sync.dma_start(
-                    out=out_rows(pl)[:, mt - 1 : mt + 1, :], in_=frame[pl][:, mt - 1 : mt + 1, :]
-                )
+            if pl == 3 and mt != 2:
+                lo = 2 if mt == 3 else mt
+                nc.sync.dma_start(out=out_rows(pl)[:, lo : mt + 1, :], in_=frame[pl][:, lo : mt + 1, :])
 
         def finish(pl):
             for mt in range(M_TILES):

@@ -45,7 +45,6 @@ def tile_locallyconnected2d_kernel(tc, inputs, kernel, bias, grad_out, out):
         stage = ctx.enter_context(tc.tile_pool(name="stage", bufs=3))
         small = ctx.enter_context(tc.tile_pool(name="small", bufs=4))
         psum = ctx.enter_context(tc.psum_pool(name="psum", bufs=8))
-        ctx.enter_context(tc.manual_schedule())
 
         raw = {}
         for who, c in LOADS:

@@ -69,7 +69,8 @@ def tile_locallyconnected2d_kernel(tc, inputs, kernel, bias, grad_out, out):
         nc.scalar.copy(out=frame[1][:, :, 2 * C : W], in_=frame[3][:, :, 0 : 2 * C])
         res0 = keep.tile([P, M_TILES, C], F32, name="res0")
 
-        nc.sync.dma_start(out=out_rows(0)[:, :, C:W], in_=frame[3][:, :, 0 : 3 * C])
+        for t in range(M_TILES):
+            nc.sync.dma_start(out=out_rows(0)[:, t, C:W], in_=frame[3][:, t, 0 : 3 * C])
 
         grouped = {}
         codes = {}
@@ -157,7 +158,8 @@ def tile_locallyconnected2d_kernel(tc, inputs, kernel, bias, grad_out, out):
             for mt in range(M_TILES):
                 finish_tile(pl, mt)
             if pl == 0:
-                nc.sync.dma_start(out=out_rows(0)[:, :, 0:C], in_=res0[:])
+                for lo, hi in ((0, 2), (2, 3), (3, 4)):
+                    nc.sync.dma_start(out=out_rows(0)[:, lo:hi, 0:C], in_=res0[:, lo:hi, :])
             else:
                 nc.sync.dma_start(
                     out=out_rows(pl).rearrange("m t f -> m (t f)"),

@@ -150,16 +150,16 @@ def tile_locallyconnected2d_kernel(tc, inputs, kernel, bias, grad_out, out):
                 mx_pass(pl, mt, 0)
             mx_pass(pl, mt, 1)
             evacuate(pl, mt)
-            if pl == 3 and mt != 2:
-                lo = 2 if mt == 3 else mt
+            if pl == 3 and mt % 2 == 1:
+                lo = mt - 1
                 nc.sync.dma_start(out=out_rows(pl)[:, lo : mt + 1, :], in_=frame[pl][:, lo : mt + 1, :])
 
         def finish(pl):
             for mt in range(M_TILES):
                 finish_tile(pl, mt)
             if pl == 0:
-                for lo, hi in ((0, 2), (2, 3), (3, 4)):
-                    nc.sync.dma_start(out=out_rows(0)[:, lo:hi, 0:C], in_=res0[:, lo:hi, :])
+                for t in range(M_TILES):
+                    nc.sync.dma_start(out=out_rows(0)[:, t, 0:C], in_=res0[:, t, :])
             else:
                 nc.sync.dma_start(
                     out=out_rows(pl).rearrange("m t f -> m (t f)"),

from contextlib import ExitStack

import concourse.mybir as mybir

B = 1024
PLACES = 4
C = 512
FLOPS = 2 * PLACES * C * C * B
BYTES = 2 * B * PLACES * C * 2 + (PLACES * C) * (PLACES * C) * 4

BF16 = mybir.dt.bfloat16
F32 = mybir.dt.float32
I32 = mybir.dt.int32
U32 = mybir.dt.uint32
U8 = mybir.dt.uint8
E4M3X4 = mybir.dt.float8_e4m3fn_x4
E5M2X4 = mybir.dt.float8_e5m2_x4

P = 128
PACK = 4
K_PASS = P * PACK
PASSES = B // K_PASS
M_TILES = C // P
W = PLACES * C

UNITS = [
    ("x", 0, 3), ("x", 0, 2),
    ("g", 0, 3), ("g", 0, 2),
    ("g", 1, 3), ("g", 1, 2),
    ("x", 1, 3),
    ("x", 1, 2),
    ("x", 0, 1), ("g", 0, 1), ("g", 1, 1), ("x", 1, 1),
    ("x", 0, 0), ("g", 0, 0), ("g", 1, 0), ("x", 1, 0),
]
LOADS = [("x", 0), ("g", 0), ("g", 1), ("x", 1)]


def tile_locallyconnected2d_kernel(tc, inputs, kernel, bias, grad_out, out):
    nc = tc.nc
    x2 = inputs.rearrange("b h w c -> b (h w c)")
    g2 = grad_out.rearrange("b h w c -> b (h w c)")
    out2 = out.rearrange("a b c d e f -> (a b c) (d e f)")
    with ExitStack() as ctx:
        keep = ctx.enter_context(tc.tile_pool(name="keep", bufs=1))
        stage = ctx.enter_context(tc.tile_pool(name="stage", bufs=3))
        small = ctx.enter_context(tc.tile_pool(name="small", bufs=4))
        psum = ctx.enter_context(tc.psum_pool(name="psum", bufs=8))

        raw = {}
        for who, c in LOADS:
            src = x2 if who == "x" else g2
            t = keep.tile([P, PACK, W], BF16, name="raw_%s%d" % (who, c))
            nc.sync.dma_start(
                out=t[:],
                in_=src[c * K_PASS : (c + 1) * K_PASS, :].rearrange("(p j) w -> p j w", j=PACK),
            )
            raw[(who, c)] = t

        def out_rows(pl):
            return out2[pl * C : (pl + 1) * C, :].rearrange("(m t) f -> m t f", t=M_TILES)

        frame = {}
        for pl in (3, 2, 1):
            frame[pl] = keep.tile([P, M_TILES, W], F32, name="frame_%d" % pl)
        nc.vector.memset(frame[3][:, :, 0 : 3 * C].bitcast(I32), 0)
        nc.scalar.copy(out=frame[2][:, :, 0 : 2 * C], in_=frame[3][:, :, 0 : 2 * C])
        nc.scalar.copy(out=frame[2][:, :, 3 * C : W], in_=frame[3][:, :, 0:C])
        nc.scalar.copy(out=frame[1][:, :, 0:C], in_=frame[3][:, :, 0:C])
        nc.scalar.copy(out=frame[1][:, :, 2 * C : W], in_=frame[3][:, :, 0 : 2 * C])
        res0 = keep.tile([P, M_TILES, C], F32, name="res0")

        for t in range(M_TILES):
            nc.sync.dma_start(out=out_rows(0)[:, t, C:W], in_=frame[3][:, t, 0 : 3 * C])

        grouped = {}
        codes = {}
        scales = {}
        acc = {}

        def regroup(u):
            who, c, pl = u
            gr = stage.tile([P, C, PACK], BF16, name="grouped", align_bytes=64)
            if who == "x":
                dst = gr[:].rearrange("p (i c) t -> p c t i", i=4)
            else:
                dst = gr[:].rearrange("p (c i) t -> p c t i", i=4)
            nc.vector.tensor_copy(
                out=dst,
                in_=raw[(who, c)][:, :, pl * C : (pl + 1) * C].rearrange("p t (c i) -> p c t i", i=4),
            )
            grouped[u] = gr

        def quantise(u):
            who, c, pl = u
            cd = keep.tile([P, C], U32, name="codes_%s%d%d" % u, align_bytes=64)
            sc = keep.tile([P, C], U8, name="scales_%s%d%d" % u, align_bytes=64)
            nc.vector.quantize_mx(
                out=cd[:].bitcast(E4M3X4 if who == "x" else E5M2X4),
                scales=sc[:],
                in_=grouped[u][:].rearrange("p w j -> p (w j)"),
            )
            codes[u] = cd
            scales[u] = sc

        def regroup_tile(mt):
            gs = small.tile([P, P, PACK], BF16, name="grouped_s", align_bytes=64)
            nc.vector.tensor_copy(
                out=gs[:],
                in_=raw[("x", 1)][:, :, 3 * C : W].rearrange("p j (m i) -> p i m j", i=4)[:, mt, :, :],
            )
            grouped[mt] = gs

        def quantise_tile(mt):
            cd = keep.tile([P, P], U32, name="codes_t%d" % mt, align_bytes=64)
            sc = keep.tile([P, P], U8, name="scales_t%d" % mt, align_bytes=64)
            nc.vector.quantize_mx(
                out=cd[:].bitcast(E4M3X4), scales=sc[:], in_=grouped[mt][:].rearrange("p w j -> p (w j)")
            )
            codes[mt] = cd
            scales[mt] = sc

        def mx_pass(pl, mt, c):
            if c == 0:
                acc[(pl, mt)] = psum.tile([P, C], F32, name="acc")
            if (c, pl) == (1, 3):
                lhs = codes[mt][:]
                lhs_scale = scales[mt][:]
            else:
                lhs = codes[("x", c, pl)][:, mt * P : (mt + 1) * P]
                lhs_scale = scales[("x", c, pl)][:, mt * P : (mt + 1) * P]
            nc.tensor.matmul_mx(
                out=acc[(pl, mt)][:],
                lhsT=lhs.bitcast(E4M3X4),
                lhsT_scale=lhs_scale,
                rhs=codes[("g", c, pl)][:].bitcast(E5M2X4),
                rhs_scale=scales[("g", c, pl)][:],
                start=(c == 0),
                stop=(c == PASSES - 1),
            )

        def evacuate(pl, mt):
            if pl == 0:
                dst = res0[:, mt, :]
            else:
                dst = frame[pl][:, mt, pl * C : (pl + 1) * C]
            nc.scalar.copy(out=dst, in_=acc[(pl, mt)][:])

        def finish_tile(pl, mt):
            if pl != 3:
                mx_pass(pl, mt, 0)
            mx_pass(pl, mt, 1)
            evacuate(pl, mt)
            if pl == 3 and mt % 2 == 1:
                lo = mt - 1
                nc.sync.dma_start(out=out_rows(pl)[:, lo : mt + 1, :], in_=frame[pl][:, lo : mt + 1, :])

        def finish(pl):
            for mt in range(M_TILES):
                finish_tile(pl, mt)
            if pl == 0:
                for t in range(M_TILES):
                    nc.sync.dma_start(out=out_rows(0)[:, t, 0:C], in_=res0[:, t, :])
            else:
                nc.sync.dma_start(
                    out=out_rows(pl).rearrange("m t f -> m (t f)"),
                    in_=frame[pl][:].rearrange("p t f -> p (t f)"),
                )

        def after(u):
            if u == ("g", 0, 3):
                for mt in range(M_TILES):
                    mx_pass(3, mt, 0)
            if u[0] == "x" and u[1] == 1:
                finish(u[2])

        def run(units):
            regroup(units[0])
            for i, u in enumerate(units):
                if i + 1 < len(units):
                    regroup(units[i + 1])
                quantise(u)
                after(u)

        cut = UNITS.index(("x", 1, 3))
        run(UNITS[:cut])
        regroup_tile(0)
        for mt in range(M_TILES):
            if mt + 1 < M_TILES:
                regroup_tile(mt + 1)
            quantise_tile(mt)
            finish_tile(3, mt)
        run(UNITS[cut + 1 :])
